import numpy as np
import ml_dtypes


def mxq(x, axis, fmt="e4m3"):
    dtype, down = {"e4m3": (ml_dtypes.float8_e4m3fn, 7), "e5m2": (ml_dtypes.float8_e5m2, 14)}[fmt]
    v = np.moveaxis(np.asarray(x, np.float32).astype(ml_dtypes.bfloat16).astype(np.float64), axis, -1)
    blocks = v.reshape(v.shape[:-1] + (-1, 32))
    amax = np.abs(blocks).max(-1, keepdims=True)
    byte = np.maximum(np.where(amax > 0, np.frexp(amax)[1] - 1 + 127, 0) - down, 1)
    scale = np.exp2(byte - 127.0)
    codes = (blocks / scale).astype(np.float32).astype(dtype).astype(np.float64)
    return np.moveaxis((codes * scale).reshape(v.shape), -1, axis)


WIDE = False


def mx_kscale(k):
    if not WIDE:
        return np.ones(k)
    levels = np.array([10, -10, 5, -5, 0])
    a = np.random.permutation(np.resize(levels, k // 512 * 4)).reshape(k // 512, 4)
    idx = np.arange(k)
    return np.exp2(a[idx // 512, idx % 128 // 32])


BF16 = ml_dtypes.bfloat16


def bf(x):
    return np.asarray(x, np.float32).astype(BF16)


def f64(x):
    return np.asarray(x).astype(np.float64)


E2M1 = np.array([0.0, 0.5, 1.0, 1.5, 2.0, 3.0, 4.0, 6.0, -0.0, -0.5, -1.0, -1.5, -2.0, -3.0, -4.0, -6.0])


def pack_weight(w, fmt):
    k, n = w.shape
    w = f64(bf(w)).reshape(k // 32, 32, n)
    amax = np.abs(w).max(1)
    if fmt == "e4m3":
        byte = np.frexp(amax)[1] - 1 + 127 - 7
    else:
        mant, ex = np.frexp(amax / 6.0)
        byte = np.where(mant > 0.5, ex, ex - 1) + 127
    byte = np.clip(np.where(amax > 0, byte, 1), 1, 254)
    scaled = (w * np.exp2(127.0 - byte)[:, None, :]).reshape(k, n).astype(np.float32)
    by_word = np.ascontiguousarray(scaled.reshape(k // 512, 128, 4, n).transpose(0, 1, 3, 2))
    if fmt == "e4m3":
        words = by_word.astype(ml_dtypes.float8_e4m3fn).view(np.uint8)
    else:
        c = by_word.astype(ml_dtypes.float4_e2m1fn).view(np.uint8) & 0xF
        words = c[..., 0::2] | (c[..., 1::2] << 4)
    return np.ascontiguousarray(words), np.ascontiguousarray(byte.astype(np.uint8).reshape(k // 512, 16, n))


def unpack_weight(words, scales, fmt):
    g, p, n, _ = words.shape
    if fmt == "e4m3":
        vals = np.ascontiguousarray(words).view(ml_dtypes.float8_e4m3fn).astype(np.float64)
    else:
        nib = np.empty((g, p, n, 4), np.uint8)
        nib[..., 0::2] = words & 0xF
        nib[..., 1::2] = words >> 4
        vals = E2M1[nib]
    vals = vals * np.repeat(np.exp2(scales.astype(np.float64) - 127.0), 8, axis=1)[..., None]
    return vals.transpose(0, 1, 3, 2).reshape(g * 512, n)

def pack4(w):
    words, scales = pack_weight(w, "e2m1")
    return words.reshape(words.shape[0], 128, -1), scales


def unpack4(words, scales):
    return unpack_weight(words.reshape(words.shape[0], 128, -1, 2), scales, "e2m1")


B, N, C = 2, 512, 1024
R = B * N
G = 3 * C


def sigmoid(v):
    return 1.0 / (1.0 + np.exp(-v))


def setup_inputs():
    s = mx_kscale(C)
    s = s / s.max()
    x_proj = bf(np.random.standard_normal((R, G)))
    annotations = bf(np.random.standard_normal((B, N, C)) * s)
    words, scales = pack4(np.random.standard_normal((C, G)) / np.sqrt(C) / s[:, None])
    bias_h = bf(np.random.standard_normal(G) * 0.3)
    return {"x_proj": x_proj,
            "annotations": annotations,
            "recurrent_kernel_words": words,
            "recurrent_kernel_scales": scales,
            "bias_h": bias_h}


def reference(x_proj, annotations, recurrent_kernel_words, recurrent_kernel_scales, bias_h):
    b, n, c = annotations.shape
    h = f64(annotations).reshape(-1, c)
    mh = (mxq(h, 1, "e4m3") @ unpack4(recurrent_kernel_words, recurrent_kernel_scales)) + f64(bias_h)
    xz, xr, xh = np.split(f64(x_proj), 3, axis=-1)
    hz, hr, hh_in = np.split(mh, 3, axis=-1)
    z = sigmoid(xz + hz)
    r = sigmoid(xr + hr)
    hh = np.tanh(xh + r * hh_in)
    out = z * h + (1.0 - z) * hh
    return out.reshape(b, n, c)

@@ -1,0 +1,278 @@
+from contextlib import ExitStack
+
+import concourse.mybir as mybir
+from concourse.masks import make_identity
+
+F32 = mybir.dt.float32
+BF16 = mybir.dt.bfloat16
+I32 = mybir.dt.int32
+U8 = mybir.dt.uint8
+U32 = mybir.dt.uint32
+E4M3_X4 = mybir.dt.float8_e4m3fn_x4
+E2M1_X4 = mybir.dt.float4_e2m1fn_x4
+ACT = mybir.ActivationFunctionType
+ALU = mybir.AluOpType
+
+P = 128
+NODES = 1024
+HIDDEN = 1024
+GATE_COLS = 3 * HIDDEN
+UPDATE, RESET, CANDIDATE = 0, 1, 2
+K_PASS = 4 * P
+PASSES = HIDDEN // K_PASS
+NODE_TILES = NODES // P
+BANK = 512
+TILES = BANK // P
+HALVES = NODES // BANK
+COLUMN_HALVES = HIDDEN // BANK
+WORDS = K_PASS // 2
+
+FLOPS = 2 * NODES * HIDDEN * GATE_COLS
+
+
+def tile_gatedgraphconvolution_pb_kernel(
+    tc, x_proj, annotations, recurrent_kernel_words, recurrent_kernel_scales, bias_h, out
+):
+    nc = tc.nc
+    x_dram = x_proj.rearrange("(p t) c -> p t c", t=NODE_TILES)
+    h_dram = annotations.flatten_outer_dims().rearrange("(p t) k -> p t k", t=NODE_TILES)
+    out_dram = out.flatten_outer_dims().rearrange("(p t) c -> p t c", t=NODE_TILES)
+
+    with ExitStack() as stack:
+        stack.enter_context(tc.manual_schedule())
+        keep = stack.enter_context(tc.tile_pool(name="keep", bufs=1))
+        stage = stack.enter_context(tc.tile_pool(name="stage", bufs=2))
+        work = stack.enter_context(tc.tile_pool(name="work", bufs=2))
+        psum_mx = stack.enter_context(tc.psum_pool(name="psum_mx", bufs=4))
+        psum_plain = stack.enter_context(tc.psum_pool(name="psum_plain", bufs=4))
+
+        x_sb = keep.tile([P, NODE_TILES, GATE_COLS], BF16)
+        h_sb = keep.tile([P, NODE_TILES, HIDDEN], BF16)
+        w_words = keep.tile([P, PASSES, 2 * GATE_COLS], U8, align_bytes=64)
+        w_scales = keep.tile([P, PASSES, GATE_COLS], U8, align_bytes=64)
+        h_codes = keep.tile([P, PASSES, NODES], U32, align_bytes=64)
+        h_scales = keep.tile([P, PASSES, NODES], U8, align_bytes=64)
+        bias_rows = keep.tile([P, P], BF16)
+        ident_f32 = keep.tile([P, P], F32)
+        ident_bf16 = keep.tile([P, P], BF16)
+
+        nc.vector.memset(bias_rows[:], 0.0)
+        nc.vector.memset(w_scales[:].bitcast(I32), 0)
+        make_identity(nc, ident_f32[:])
+        make_identity(nc, ident_bf16[:])
+
+        for t in range(TILES):
+            nc.sync.dma_start(out=h_sb[:, t, :], in_=h_dram[:, t, :])
+        nc.sync.dma_start(
+            out=bias_rows[0 : GATE_COLS // P, :], in_=bias_h.rearrange("(m c) -> m c", c=P)
+        )
+        for b in range(2):
+            for r in range(4):
+                nc.sync.dma_start(
+                    out=w_scales[32 * b + r : P : 64, :, :].bitcast(I32),
+                    in_=recurrent_kernel_scales[:, 4 * b + r : 16 : 8, :]
+                    .rearrange("g s n -> s g n")
+                    .bitcast(I32),
+                )
+        for gate in (RESET, CANDIDATE, UPDATE):
+            gate_bytes = slice(2 * HIDDEN * gate, 2 * HIDDEN * (gate + 1))
+            nc.sync.dma_start(
+                out=w_words[:, :, gate_bytes].bitcast(I32),
+                in_=recurrent_kernel_words[:, :, gate_bytes].rearrange("g p b -> p g b").bitcast(I32),
+            )
+        for t in range(TILES):
+            nc.sync.dma_start(out=x_sb[:, t, :], in_=x_dram[:, t, :])
+        nc.sync.dma_start(out=h_sb[:, TILES:, :], in_=h_dram[:, TILES:, :])
+        for t in range(TILES, NODE_TILES):
+            nc.sync.dma_start(out=x_sb[:, t, :], in_=x_dram[:, t, :])
+
+        h_words = h_sb[:].bitcast(F32)
+
+        def quantise_half(half):
+            nodes = slice(BANK * half, BANK * (half + 1))
+            for g in range(PASSES):
+                grouped = stage.tile([P, BANK, 4], BF16, align_bytes=64)
+                grouped_words = grouped[:].bitcast(F32)
+                for pair in range(TILES // 2):
+                    turned = psum_plain.tile([P, 2, 2, P], F32, tag="plain")
+                    for a in range(2):
+                        t = TILES * half + 2 * pair + a
+                        for u in range(2):
+                            nc.tensor.transpose(
+                                turned[:, a, u, :],
+                                h_words[:, t, WORDS * g + u : WORDS * (g + 1) : 2],
+                                ident_f32[:],
+                            )
+                    nc.scalar.copy(
+                        out=grouped_words[:, 2 * P * pair : 2 * P * (pair + 1), :].rearrange(
+                            "p (a m) u -> p a m u", a=2
+                        ),
+                        in_=turned[:].rearrange("p a u m -> p a m u"),
+                    )
+                nc.vector.quantize_mx(
+                    out=h_codes[:, g, nodes].bitcast(E4M3_X4),
+                    scales=h_scales[:, g, nodes],
+                    in_=grouped[:].rearrange("p n f -> p (n f)"),
+                )
+
+        quantise_half(0)
+
+        bias_turned = psum_plain.tile([P, P], BF16, tag="plain")
+        nc.tensor.transpose(bias_turned[:], bias_rows[:], ident_bf16[:])
+        bias_col = keep.tile([P, GATE_COLS // P], F32)
+        nc.vector.tensor_copy(out=bias_col[:], in_=bias_turned[:, 0 : GATE_COLS // P])
+        first_cand_tile = HIDDEN * CANDIDATE // P
+        cand_bias_col = keep.tile([P, HIDDEN // P], BF16)
+        nc.vector.tensor_copy(
+            out=cand_bias_col[:], in_=bias_turned[:, first_cand_tile : first_cand_tile + HIDDEN // P]
+        )
+        cand_bias = keep.tile([P, HIDDEN], F32)
+        for q in range(COLUMN_HALVES):
+            spread = psum_plain.tile([P, BANK], F32, tag="plain")
+            for ct in range(TILES):
+                nc.tensor.matmul(
+                    out=spread[:, P * ct : P * (ct + 1)],
+                    lhsT=cand_bias_col[:, TILES * q + ct : TILES * q + ct + 1].to_broadcast([P, P]),
+                    rhs=ident_bf16[:],
+                    start=True,
+                    stop=True,
+                )
+            nc.vector.tensor_copy(out=cand_bias[:, BANK * q : BANK * (q + 1)], in_=spread[:])
+
+        def gate_transposed(gate, half, q):
+            nodes = slice(BANK * half, BANK * (half + 1))
+            pre_t = work.tile([P, TILES, BANK], F32, tag="pre_t_%d" % gate)
+            for ct in range(TILES):
+                col = HIDDEN * gate + BANK * q + P * ct
+                acc = psum_mx.tile([P, BANK], F32, tag="mx")
+                for g in range(PASSES):
+                    nc.tensor.matmul_mx(
+                        out=acc[:],
+                        lhsT=w_words[:, g, 2 * col : 2 * (col + P)].bitcast(E2M1_X4),
+                        lhsT_scale=w_scales[:, g, col : col + P],
+                        rhs=h_codes[:, g, nodes].bitcast(E4M3_X4),
+                        rhs_scale=h_scales[:, g, nodes],
+                        start=(g == 0),
+                        stop=(g == PASSES - 1),
+                    )
+                nc.scalar.activation(
+                    out=pre_t[:, ct, :],
+                    in_=acc[:],
+                    func=ACT.Identity,
+                    bias=bias_col[:, col // P : col // P + 1],
+                    scale=1.0,
+                )
+            return pre_t
+
+        def gate_on_nodes(pre_t, gate, half, q):
+            col = HIDDEN * gate + BANK * q
+            values = work.tile([P, TILES, BANK], F32, tag="gate_%d" % gate)
+            for j in range(TILES):
+                pre = psum_plain.tile([P, BANK], F32, tag="plain")
+                for ct in range(TILES):
+                    nc.tensor.matmul(
+                        out=pre[:, P * ct : P * (ct + 1)],
+                        lhsT=pre_t[:, ct, P * j : P * (j + 1)],
+                        rhs=ident_f32[:],
+                        is_transpose=True,
+                        start=(ct == 0),
+                        stop=False,
+                    )
+                nc.tensor.matmul(
+                    out=pre[:],
+                    lhsT=ident_bf16[:],
+                    rhs=x_sb[:, TILES * half + j, col : col + BANK],
+                    start=False,
+                    stop=True,
+                )
+                nc.scalar.activation(out=values[:, j, :], in_=pre[:], func=ACT.Sigmoid)
+            return values
+
+        def candidate_recurrent(half, q):
+            col = HIDDEN * CANDIDATE + BANK * q
+            cand = work.tile([P, TILES, BANK], F32, tag="cand")
+            for j in range(TILES):
+                nodes = slice(P * (TILES * half + j), P * (TILES * half + j + 1))
+                acc = psum_mx.tile([P, BANK], F32, tag="mx")
+                for g in range(PASSES):
+                    nc.tensor.matmul_mx(
+                        out=acc[:],
+                        lhsT=h_codes[:, g, nodes].bitcast(E4M3_X4),
+                        lhsT_scale=h_scales[:, g, nodes],
+                        rhs=w_words[:, g, 2 * col : 2 * (col + BANK)].bitcast(E2M1_X4),
+                        rhs_scale=w_scales[:, g, col : col + BANK],
+                        start=(g == 0),
+                        stop=(g == PASSES - 1),
+                    )
+                nc.vector.tensor_tensor(
+                    out=cand[:, j, :],
+                    in0=acc[:],
+                    in1=cand_bias[:, BANK * q : BANK * (q + 1)],
+                    op=ALU.add,
+                )
+            return cand
+
+        pair_starts = range(0, TILES, 2)
+
+        def candidate_input(cand, reset, half, q):
+            col = HIDDEN * CANDIDATE + BANK * q
+            for first in pair_starts:
+                rows = slice(first, first + 2)
+                nc.vector.tensor_tensor(
+                    out=cand[:, rows, :], in0=cand[:, rows, :], in1=reset[:, rows, :], op=ALU.mult
+                )
+            for first in pair_starts:
+                rows = slice(first, first + 2)
+                tiles = slice(TILES * half + first, TILES * half + first + 2)
+                nc.vector.tensor_tensor(
+                    out=cand[:, rows, :],
+                    in0=cand[:, rows, :],
+                    in1=x_sb[:, tiles, col : col + BANK],
+                    op=ALU.add,
+                )
+
+        def squash(cand):
+            for first in pair_starts:
+                rows = slice(first, first + 2)
+                nc.scalar.activation(out=cand[:, rows, :], in_=cand[:, rows, :], func=ACT.Tanh)
+
+        def mix_and_store(cand, update, half, q):
+            cols = slice(BANK * q, BANK * (q + 1))
+            mixed = work.tile([P, TILES, BANK], F32, tag="mixed")
+            for first in pair_starts:
+                rows = slice(first, first + 2)
+                tiles = slice(TILES * half + first, TILES * half + first + 2)
+                nc.vector.tensor_tensor(
+                    out=mixed[:, rows, :], in0=h_sb[:, tiles, cols], in1=cand[:, rows, :], op=ALU.subtract
+                )
+            for first in pair_starts:
+                rows = slice(first, first + 2)
+                nc.vector.tensor_tensor(
+                    out=mixed[:, rows, :], in0=mixed[:, rows, :], in1=update[:, rows, :], op=ALU.mult
+                )
+            for first in pair_starts:
+                rows = slice(first, first + 2)
+                tiles = slice(TILES * half + first, TILES * half + first + 2)
+                nc.vector.tensor_tensor(
+                    out=mixed[:, rows, :], in0=mixed[:, rows, :], in1=cand[:, rows, :], op=ALU.add
+                )
+                nc.sync.dma_start(out=out_dram[:, tiles, cols], in_=mixed[:, rows, :])
+
+        waiting = None
+        for half in range(HALVES):
+            for q in range(COLUMN_HALVES):
+                reset_t = gate_transposed(RESET, half, q)
+                if waiting is not None:
+                    squash(waiting[0])
+                cand = candidate_recurrent(half, q)
+                update_t = gate_transposed(UPDATE, half, q)
+                if waiting is not None:
+                    mix_and_store(*waiting)
+                reset = gate_on_nodes(reset_t, RESET, half, q)
+                update = gate_on_nodes(update_t, UPDATE, half, q)
+                candidate_input(cand, reset, half, q)
+                if q == 0 and half + 1 < HALVES:
+                    quantise_half(half + 1)
+                waiting = (cand, update, half, q)
+        squash(waiting[0])
+        mix_and_store(*waiting)

@@ -56,10 +56,25 @@ def tile_gatedgraphconvolution_pb_kernel(
         ident_f32 = keep.tile([P, P], F32)
         ident_bf16 = keep.tile([P, P], BF16)
 
+        table_warmer = keep.tile([P, 1], F32)
+        nc.vector.memset(table_warmer[:], 0.0)
+        nc.scalar.activation(out=table_warmer[:], in_=table_warmer[:], func=ACT.Sigmoid)
         nc.vector.memset(bias_rows[:], 0.0)
         nc.vector.memset(w_scales[:].bitcast(I32), 0)
         make_identity(nc, ident_f32[:])
         make_identity(nc, ident_bf16[:])
+
+        def load_w(gate):
+            gate_bytes = slice(2 * HIDDEN * gate, 2 * HIDDEN * (gate + 1))
+            nc.sync.dma_start(
+                out=w_words[:, :, gate_bytes].bitcast(I32),
+                in_=recurrent_kernel_words[:, :, gate_bytes].rearrange("g p b -> p g b").bitcast(I32),
+            )
+
+        def load_x(gate, half):
+            tiles = slice(TILES * half, TILES * (half + 1))
+            cols = slice(HIDDEN * gate, HIDDEN * (gate + 1))
+            nc.sync.dma_start(out=x_sb[:, tiles, cols], in_=x_dram[:, tiles, cols])
 
         for t in range(TILES):
             nc.sync.dma_start(out=h_sb[:, t, :], in_=h_dram[:, t, :])
@@ -74,48 +89,47 @@ def tile_gatedgraphconvolution_pb_kernel(
                     .rearrange("g s n -> s g n")
                     .bitcast(I32),
                 )
-        for gate in (RESET, CANDIDATE, UPDATE):
-            gate_bytes = slice(2 * HIDDEN * gate, 2 * HIDDEN * (gate + 1))
-            nc.sync.dma_start(
-                out=w_words[:, :, gate_bytes].bitcast(I32),
-                in_=recurrent_kernel_words[:, :, gate_bytes].rearrange("g p b -> p g b").bitcast(I32),
-            )
-        for t in range(TILES):
-            nc.sync.dma_start(out=x_sb[:, t, :], in_=x_dram[:, t, :])
+        load_w(RESET)
+        load_w(CANDIDATE)
+        load_x(RESET, 0)
+        load_w(UPDATE)
+        load_x(CANDIDATE, 0)
+        load_x(UPDATE, 0)
         nc.sync.dma_start(out=h_sb[:, TILES:, :], in_=h_dram[:, TILES:, :])
-        for t in range(TILES, NODE_TILES):
-            nc.sync.dma_start(out=x_sb[:, t, :], in_=x_dram[:, t, :])
+        load_x(RESET, 1)
+        load_x(CANDIDATE, 1)
+        load_x(UPDATE, 1)
 
         h_words = h_sb[:].bitcast(F32)
 
-        def quantise_half(half):
+        def turn_half(half):
+            grouped = stage.tile([P, PASSES, BANK, 4], BF16, align_bytes=64)
+            grouped_words = grouped[:].bitcast(F32)
+            for j in range(TILES):
+                turned = psum_plain.tile([P, PASSES, 2, P], F32, tag="plain")
+                for g in range(PASSES):
+                    for u in range(2):
+                        nc.tensor.transpose(
+                            turned[:, g, u, :],
+                            h_words[:, TILES * half + j, WORDS * g + u : WORDS * (g + 1) : 2],
+                            ident_f32[:],
+                        )
+                nc.scalar.copy(
+                    out=grouped_words[:, :, P * j : P * (j + 1), :],
+                    in_=turned[:].rearrange("p g u m -> p g m u"),
+                )
+            return grouped
+
+        def quantise_half(grouped, half):
             nodes = slice(BANK * half, BANK * (half + 1))
             for g in range(PASSES):
-                grouped = stage.tile([P, BANK, 4], BF16, align_bytes=64)
-                grouped_words = grouped[:].bitcast(F32)
-                for pair in range(TILES // 2):
-                    turned = psum_plain.tile([P, 2, 2, P], F32, tag="plain")
-                    for a in range(2):
-                        t = TILES * half + 2 * pair + a
-                        for u in range(2):
-                            nc.tensor.transpose(
-                                turned[:, a, u, :],
-                                h_words[:, t, WORDS * g + u : WORDS * (g + 1) : 2],
-                                ident_f32[:],
-                            )
-                    nc.scalar.copy(
-                        out=grouped_words[:, 2 * P * pair : 2 * P * (pair + 1), :].rearrange(
-                            "p (a m) u -> p a m u", a=2
-                        ),
-                        in_=turned[:].rearrange("p a u m -> p a m u"),
-                    )
                 nc.vector.quantize_mx(
                     out=h_codes[:, g, nodes].bitcast(E4M3_X4),
                     scales=h_scales[:, g, nodes],
-                    in_=grouped[:].rearrange("p n f -> p (n f)"),
+                    in_=grouped[:, g, :, :].rearrange("p n f -> p (n f)"),
                 )
 
-        quantise_half(0)
+        grouped_0 = turn_half(0)
 
         bias_turned = psum_plain.tile([P, P], BF16, tag="plain")
         nc.tensor.transpose(bias_turned[:], bias_rows[:], ident_bf16[:])
@@ -127,8 +141,10 @@ def tile_gatedgraphconvolution_pb_kernel(
             out=cand_bias_col[:], in_=bias_turned[:, first_cand_tile : first_cand_tile + HIDDEN // P]
         )
         cand_bias = keep.tile([P, HIDDEN], F32)
+        spreads = []
         for q in range(COLUMN_HALVES):
             spread = psum_plain.tile([P, BANK], F32, tag="plain")
+            spreads.append(spread)
             for ct in range(TILES):
                 nc.tensor.matmul(
                     out=spread[:, P * ct : P * (ct + 1)],
@@ -137,7 +153,10 @@ def tile_gatedgraphconvolution_pb_kernel(
                     start=True,
                     stop=True,
                 )
-            nc.vector.tensor_copy(out=cand_bias[:, BANK * q : BANK * (q + 1)], in_=spread[:])
+
+        quantise_half(grouped_0, 0)
+        for q in range(COLUMN_HALVES):
+            nc.vector.tensor_copy(out=cand_bias[:, BANK * q : BANK * (q + 1)], in_=spreads[q][:])
 
         def gate_transposed(gate, half, q):
             nodes = slice(BANK * half, BANK * (half + 1))
@@ -258,21 +277,15 @@ def tile_gatedgraphconvolution_pb_kernel(
                 )
                 nc.sync.dma_start(out=out_dram[:, tiles, cols], in_=mixed[:, rows, :])
 
-        waiting = None
         for half in range(HALVES):
             for q in range(COLUMN_HALVES):
                 reset_t = gate_transposed(RESET, half, q)
-                if waiting is not None:
-                    squash(waiting[0])
                 cand = candidate_recurrent(half, q)
-                update_t = gate_transposed(UPDATE, half, q)
-                if waiting is not None:
-                    mix_and_store(*waiting)
                 reset = gate_on_nodes(reset_t, RESET, half, q)
-                update = gate_on_nodes(update_t, UPDATE, half, q)
+                update_t = gate_transposed(UPDATE, half, q)
                 candidate_input(cand, reset, half, q)
+                squash(cand)
+                update = gate_on_nodes(update_t, UPDATE, half, q)
+                mix_and_store(cand, update, half, q)
                 if q == 0 and half + 1 < HALVES:
-                    quantise_half(half + 1)
-                waiting = (cand, update, half, q)
-        squash(waiting[0])
-        mix_and_store(*waiting)
+                    quantise_half(turn_half(half + 1), half + 1)

@@ -46,12 +46,19 @@ def tile_gatedgraphconvolution_pb_kernel(
         psum_mx = stack.enter_context(tc.psum_pool(name="psum_mx", bufs=4))
         psum_plain = stack.enter_context(tc.psum_pool(name="psum_plain", bufs=4))
 
-        x_sb = keep.tile([P, NODE_TILES, GATE_COLS], BF16)
         h_sb = keep.tile([P, NODE_TILES, HIDDEN], BF16)
-        w_words = keep.tile([P, PASSES, 2 * GATE_COLS], U8, align_bytes=64)
+        x_sb = {}
+        w_words = {}
+        h_codes = {}
+        h_scales = {}
+        for gate in (UPDATE, RESET, CANDIDATE):
+            w_words[gate] = keep.tile([P, PASSES, 2 * HIDDEN], U8, align_bytes=64, name="w_words_%d" % gate)
+            for half in range(HALVES):
+                x_sb[gate, half] = keep.tile([P, TILES, HIDDEN], BF16, name="x_%d_%d" % (gate, half))
+        for half in range(HALVES):
+            h_codes[half] = keep.tile([P, PASSES, BANK], U32, align_bytes=64, name="h_codes_%d" % half)
+            h_scales[half] = keep.tile([P, PASSES, BANK], U8, align_bytes=64, name="h_scales_%d" % half)
         w_scales = keep.tile([P, PASSES, GATE_COLS], U8, align_bytes=64)
-        h_codes = keep.tile([P, PASSES, NODES], U32, align_bytes=64)
-        h_scales = keep.tile([P, PASSES, NODES], U8, align_bytes=64)
         bias_rows = keep.tile([P, P], BF16)
         ident_f32 = keep.tile([P, P], F32)
         ident_bf16 = keep.tile([P, P], BF16)
@@ -67,14 +74,14 @@ def tile_gatedgraphconvolution_pb_kernel(
         def load_w(gate):
             gate_bytes = slice(2 * HIDDEN * gate, 2 * HIDDEN * (gate + 1))
             nc.sync.dma_start(
-                out=w_words[:, :, gate_bytes].bitcast(I32),
+                out=w_words[gate][:].bitcast(I32),
                 in_=recurrent_kernel_words[:, :, gate_bytes].rearrange("g p b -> p g b").bitcast(I32),
             )
 
         def load_x(gate, half):
             tiles = slice(TILES * half, TILES * (half + 1))
             cols = slice(HIDDEN * gate, HIDDEN * (gate + 1))
-            nc.sync.dma_start(out=x_sb[:, tiles, cols], in_=x_dram[:, tiles, cols])
+            nc.sync.dma_start(out=x_sb[gate, half][:], in_=x_dram[:, tiles, cols])
 
         for t in range(TILES):
             nc.sync.dma_start(out=h_sb[:, t, :], in_=h_dram[:, t, :])
@@ -121,11 +128,10 @@ def tile_gatedgraphconvolution_pb_kernel(
             return grouped
 
         def quantise_half(grouped, half):
-            nodes = slice(BANK * half, BANK * (half + 1))
             for g in range(PASSES):
                 nc.vector.quantize_mx(
-                    out=h_codes[:, g, nodes].bitcast(E4M3_X4),
-                    scales=h_scales[:, g, nodes],
+                    out=h_codes[half][:, g, :].bitcast(E4M3_X4),
+                    scales=h_scales[half][:, g, :],
                     in_=grouped[:, g, :, :].rearrange("p n f -> p (n f)"),
                 )
 
@@ -159,18 +165,18 @@ def tile_gatedgraphconvolution_pb_kernel(
             nc.vector.tensor_copy(out=cand_bias[:, BANK * q : BANK * (q + 1)], in_=spreads[q][:])
 
         def gate_transposed(gate, half, q):
-            nodes = slice(BANK * half, BANK * (half + 1))
             pre_t = work.tile([P, TILES, BANK], F32, tag="pre_t_%d" % gate)
             for ct in range(TILES):
-                col = HIDDEN * gate + BANK * q + P * ct
+                col = BANK * q + P * ct
+                tile_of_w = (HIDDEN * gate + col) // P
                 acc = psum_mx.tile([P, BANK], F32, tag="mx")
                 for g in range(PASSES):
                     nc.tensor.matmul_mx(
                         out=acc[:],
-                        lhsT=w_words[:, g, 2 * col : 2 * (col + P)].bitcast(E2M1_X4),
-                        lhsT_scale=w_scales[:, g, col : col + P],
-                        rhs=h_codes[:, g, nodes].bitcast(E4M3_X4),
-                        rhs_scale=h_scales[:, g, nodes],
+                        lhsT=w_words[gate][:, g, 2 * col : 2 * (col + P)].bitcast(E2M1_X4),
+                        lhsT_scale=w_scales[:, g, P * tile_of_w : P * (tile_of_w + 1)],
+                        rhs=h_codes[half][:, g, :].bitcast(E4M3_X4),
+                        rhs_scale=h_scales[half][:, g, :],
                         start=(g == 0),
                         stop=(g == PASSES - 1),
                     )
@@ -178,13 +184,13 @@ def tile_gatedgraphconvolution_pb_kernel(
                     out=pre_t[:, ct, :],
                     in_=acc[:],
                     func=ACT.Identity,
-                    bias=bias_col[:, col // P : col // P + 1],
+                    bias=bias_col[:, tile_of_w : tile_of_w + 1],
                     scale=1.0,
                 )
             return pre_t
 
         def gate_on_nodes(pre_t, gate, half, q):
-            col = HIDDEN * gate + BANK * q
+            cols = slice(BANK * q, BANK * (q + 1))
             values = work.tile([P, TILES, BANK], F32, tag="gate_%d" % gate)
             for j in range(TILES):
                 pre = psum_plain.tile([P, BANK], F32, tag="plain")
@@ -200,7 +206,7 @@ def tile_gatedgraphconvolution_pb_kernel(
                 nc.tensor.matmul(
                     out=pre[:],
                     lhsT=ident_bf16[:],
-                    rhs=x_sb[:, TILES * half + j, col : col + BANK],
+                    rhs=x_sb[gate, half][:, j, cols],
                     start=False,
                     stop=True,
                 )
@@ -208,18 +214,18 @@ def tile_gatedgraphconvolution_pb_kernel(
             return values
 
         def candidate_recurrent(half, q):
-            col = HIDDEN * CANDIDATE + BANK * q
+            col = BANK * q
             cand = work.tile([P, TILES, BANK], F32, tag="cand")
             for j in range(TILES):
-                nodes = slice(P * (TILES * half + j), P * (TILES * half + j + 1))
+                nodes = slice(P * j, P * (j + 1))
                 acc = psum_mx.tile([P, BANK], F32, tag="mx")
                 for g in range(PASSES):
                     nc.tensor.matmul_mx(
                         out=acc[:],
-                        lhsT=h_codes[:, g, nodes].bitcast(E4M3_X4),
-                        lhsT_scale=h_scales[:, g, nodes],
-                        rhs=w_words[:, g, 2 * col : 2 * (col + BANK)].bitcast(E2M1_X4),
-                        rhs_scale=w_scales[:, g, col : col + BANK],
+                        lhsT=h_codes[half][:, g, nodes].bitcast(E4M3_X4),
+                        lhsT_scale=h_scales[half][:, g, nodes],
+                        rhs=w_words[CANDIDATE][:, g, 2 * col : 2 * (col + BANK)].bitcast(E2M1_X4),
+                        rhs_scale=w_scales[:, g, HIDDEN * CANDIDATE + col : HIDDEN * CANDIDATE + col + BANK],
                         start=(g == 0),
                         stop=(g == PASSES - 1),
                     )
@@ -234,7 +240,7 @@ def tile_gatedgraphconvolution_pb_kernel(
         pair_starts = range(0, TILES, 2)
 
         def candidate_input(cand, reset, half, q):
-            col = HIDDEN * CANDIDATE + BANK * q
+            cols = slice(BANK * q, BANK * (q + 1))
             for first in pair_starts:
                 rows = slice(first, first + 2)
                 nc.vector.tensor_tensor(
@@ -242,11 +248,10 @@ def tile_gatedgraphconvolution_pb_kernel(
                 )
             for first in pair_starts:
                 rows = slice(first, first + 2)
-                tiles = slice(TILES * half + first, TILES * half + first + 2)
                 nc.vector.tensor_tensor(
                     out=cand[:, rows, :],
                     in0=cand[:, rows, :],
-                    in1=x_sb[:, tiles, col : col + BANK],
+                    in1=x_sb[CANDIDATE, half][:, rows, cols],
                     op=ALU.add,
                 )
 

@@ -24,8 +24,15 @@ NODE_TILES = NODES // P
 BANK = 512
 TILES = BANK // P
 HALVES = NODES // BANK
-COLUMN_HALVES = HIDDEN // BANK
 WORDS = K_PASS // 2
+X_COLS = 512
+
+COL_TILES = 2
+ROUND_COLS = P * COL_TILES
+ROUNDS_PER_HALF = HIDDEN // ROUND_COLS
+ROUNDS = HALVES * ROUNDS_PER_HALF
+TILES_PER_BANK = BANK // ROUND_COLS
+ROUND_BANKS = TILES // TILES_PER_BANK
 
 FLOPS = 2 * NODES * HIDDEN * GATE_COLS
 
@@ -43,6 +50,7 @@ def tile_gatedgraphconvolution_pb_kernel(
         keep = stack.enter_context(tc.tile_pool(name="keep", bufs=1))
         stage = stack.enter_context(tc.tile_pool(name="stage", bufs=2))
         work = stack.enter_context(tc.tile_pool(name="work", bufs=2))
+        longer = stack.enter_context(tc.tile_pool(name="longer", bufs=3))
         psum_mx = stack.enter_context(tc.psum_pool(name="psum_mx", bufs=4))
         psum_plain = stack.enter_context(tc.psum_pool(name="psum_plain", bufs=4))
 
@@ -54,7 +62,10 @@ def tile_gatedgraphconvolution_pb_kernel(
         for gate in (UPDATE, RESET, CANDIDATE):
             w_words[gate] = keep.tile([P, PASSES, 2 * HIDDEN], U8, align_bytes=64, name="w_words_%d" % gate)
             for half in range(HALVES):
-                x_sb[gate, half] = keep.tile([P, TILES, HIDDEN], BF16, name="x_%d_%d" % (gate, half))
+                for block in range(HIDDEN // X_COLS):
+                    x_sb[gate, half, block] = keep.tile(
+                        [P, TILES, X_COLS], BF16, name="x_%d_%d_%d" % (gate, half, block)
+                    )
         for half in range(HALVES):
             h_codes[half] = keep.tile([P, PASSES, BANK], U32, align_bytes=64, name="h_codes_%d" % half)
             h_scales[half] = keep.tile([P, PASSES, BANK], U8, align_bytes=64, name="h_scales_%d" % half)
@@ -78,10 +89,10 @@ def tile_gatedgraphconvolution_pb_kernel(
                 in_=recurrent_kernel_words[:, :, gate_bytes].rearrange("g p b -> p g b").bitcast(I32),
             )
 
-        def load_x(gate, half):
+        def load_x(gate, half, block):
             tiles = slice(TILES * half, TILES * (half + 1))
-            cols = slice(HIDDEN * gate, HIDDEN * (gate + 1))
-            nc.sync.dma_start(out=x_sb[gate, half][:], in_=x_dram[:, tiles, cols])
+            first = HIDDEN * gate + X_COLS * block
+            nc.sync.dma_start(out=x_sb[gate, half, block][:], in_=x_dram[:, tiles, first : first + X_COLS])
 
         for t in range(TILES):
             nc.sync.dma_start(out=h_sb[:, t, :], in_=h_dram[:, t, :])
@@ -97,200 +108,215 @@ def tile_gatedgraphconvolution_pb_kernel(
                     .bitcast(I32),
                 )
         load_w(RESET)
-        load_w(CANDIDATE)
-        load_x(RESET, 0)
+        load_x(RESET, 0, 0)
         load_w(UPDATE)
-        load_x(CANDIDATE, 0)
-        load_x(UPDATE, 0)
+        load_x(UPDATE, 0, 0)
+        load_w(CANDIDATE)
+        load_x(CANDIDATE, 0, 0)
+        load_x(RESET, 0, 1)
         nc.sync.dma_start(out=h_sb[:, TILES:, :], in_=h_dram[:, TILES:, :])
-        load_x(RESET, 1)
-        load_x(CANDIDATE, 1)
-        load_x(UPDATE, 1)
+        load_x(UPDATE, 0, 1)
+        load_x(CANDIDATE, 0, 1)
+        for block in range(HIDDEN // X_COLS):
+            load_x(RESET, 1, block)
+            load_x(UPDATE, 1, block)
+            load_x(CANDIDATE, 1, block)
 
         h_words = h_sb[:].bitcast(F32)
+        grouped = {}
 
-        def turn_half(half):
-            grouped = stage.tile([P, PASSES, BANK, 4], BF16, align_bytes=64)
-            grouped_words = grouped[:].bitcast(F32)
-            for j in range(TILES):
-                turned = psum_plain.tile([P, PASSES, 2, P], F32, tag="plain")
-                for g in range(PASSES):
-                    for u in range(2):
-                        nc.tensor.transpose(
-                            turned[:, g, u, :],
-                            h_words[:, TILES * half + j, WORDS * g + u : WORDS * (g + 1) : 2],
-                            ident_f32[:],
-                        )
-                nc.scalar.copy(
-                    out=grouped_words[:, :, P * j : P * (j + 1), :],
-                    in_=turned[:].rearrange("p g u m -> p g m u"),
-                )
-            return grouped
+        def turn_tile(half, j):
+            if j == 0:
+                grouped[half] = stage.tile([P, PASSES, BANK, 4], BF16, align_bytes=64, name="grouped")
+            grouped_words = grouped[half][:].bitcast(F32)
+            turned = psum_plain.tile([P, PASSES, 2, P], F32, tag="plain")
+            for g in range(PASSES):
+                for u in range(2):
+                    nc.tensor.transpose(
+                        turned[:, g, u, :],
+                        h_words[:, TILES * half + j, WORDS * g + u : WORDS * (g + 1) : 2],
+                        ident_f32[:],
+                    )
+            nc.scalar.copy(
+                out=grouped_words[:, :, P * j : P * (j + 1), :],
+                in_=turned[:].rearrange("p g u m -> p g m u"),
+            )
 
-        def quantise_half(grouped, half):
+        def quantise_half(half):
             for g in range(PASSES):
                 nc.vector.quantize_mx(
                     out=h_codes[half][:, g, :].bitcast(E4M3_X4),
                     scales=h_scales[half][:, g, :],
-                    in_=grouped[:, g, :, :].rearrange("p n f -> p (n f)"),
+                    in_=grouped[half][:, g, :, :].rearrange("p n f -> p (n f)"),
                 )
 
-        grouped_0 = turn_half(0)
+        for j in range(TILES):
+            turn_tile(0, j)
 
         bias_turned = psum_plain.tile([P, P], BF16, tag="plain")
         nc.tensor.transpose(bias_turned[:], bias_rows[:], ident_bf16[:])
         bias_col = keep.tile([P, GATE_COLS // P], F32)
         nc.vector.tensor_copy(out=bias_col[:], in_=bias_turned[:, 0 : GATE_COLS // P])
-        first_cand_tile = HIDDEN * CANDIDATE // P
-        cand_bias_col = keep.tile([P, HIDDEN // P], BF16)
-        nc.vector.tensor_copy(
-            out=cand_bias_col[:], in_=bias_turned[:, first_cand_tile : first_cand_tile + HIDDEN // P]
-        )
-        cand_bias = keep.tile([P, HIDDEN], F32)
-        spreads = []
-        for q in range(COLUMN_HALVES):
-            spread = psum_plain.tile([P, BANK], F32, tag="plain")
-            spreads.append(spread)
-            for ct in range(TILES):
-                nc.tensor.matmul(
-                    out=spread[:, P * ct : P * (ct + 1)],
-                    lhsT=cand_bias_col[:, TILES * q + ct : TILES * q + ct + 1].to_broadcast([P, P]),
-                    rhs=ident_bf16[:],
-                    start=True,
-                    stop=True,
+        quantise_half(0)
+
+        def place(rnd):
+            return rnd // ROUNDS_PER_HALF, ROUND_COLS * (rnd % ROUNDS_PER_HALF)
+
+        def x_of(gate, rnd, j):
+            half, col = place(rnd)
+            return x_sb[gate, half, col // X_COLS][:, j, col % X_COLS : col % X_COLS + ROUND_COLS]
+
+        def bias_of(gate, col):
+            tile_of_w = (HIDDEN * gate + col) // P
+            return bias_col[:, tile_of_w : tile_of_w + 1]
+
+        def product_transposed(gate, half, col):
+            in_w = HIDDEN * gate + col
+            acc = psum_mx.tile([P, BANK], F32, tag="mx")
+            for g in range(PASSES):
+                nc.tensor.matmul_mx(
+                    out=acc[:],
+                    lhsT=w_words[gate][:, g, 2 * col : 2 * (col + P)].bitcast(E2M1_X4),
+                    lhsT_scale=w_scales[:, g, in_w : in_w + P],
+                    rhs=h_codes[half][:, g, :].bitcast(E4M3_X4),
+                    rhs_scale=h_scales[half][:, g, :],
+                    start=(g == 0),
+                    stop=(g == PASSES - 1),
                 )
+            return acc
 
-        quantise_half(grouped_0, 0)
-        for q in range(COLUMN_HALVES):
-            nc.vector.tensor_copy(out=cand_bias[:, BANK * q : BANK * (q + 1)], in_=spreads[q][:])
-
-        def gate_transposed(gate, half, q):
-            pre_t = work.tile([P, TILES, BANK], F32, tag="pre_t_%d" % gate)
-            for ct in range(TILES):
-                col = BANK * q + P * ct
-                tile_of_w = (HIDDEN * gate + col) // P
-                acc = psum_mx.tile([P, BANK], F32, tag="mx")
-                for g in range(PASSES):
-                    nc.tensor.matmul_mx(
-                        out=acc[:],
-                        lhsT=w_words[gate][:, g, 2 * col : 2 * (col + P)].bitcast(E2M1_X4),
-                        lhsT_scale=w_scales[:, g, P * tile_of_w : P * (tile_of_w + 1)],
-                        rhs=h_codes[half][:, g, :].bitcast(E4M3_X4),
-                        rhs_scale=h_scales[half][:, g, :],
-                        start=(g == 0),
-                        stop=(g == PASSES - 1),
+        def back_on_nodes(transposed, gate, rnd, func, values):
+            for bank in range(ROUND_BANKS):
+                pre = psum_plain.tile([P, TILES_PER_BANK, ROUND_COLS], F32, tag="plain")
+                for i in range(TILES_PER_BANK):
+                    j = TILES_PER_BANK * bank + i
+                    for ct in range(COL_TILES):
+                        nc.tensor.matmul(
+                            out=pre[:, i, P * ct : P * (ct + 1)],
+                            lhsT=transposed[:, ct, P * j : P * (j + 1)],
+                            rhs=ident_f32[:],
+                            is_transpose=True,
+                            start=(ct == 0),
+                            stop=False,
+                        )
+                    nc.tensor.matmul(
+                        out=pre[:, i, :], lhsT=ident_bf16[:], rhs=x_of(gate, rnd, j), start=False, stop=True
                     )
+                rows = slice(TILES_PER_BANK * bank, TILES_PER_BANK * (bank + 1))
+                nc.scalar.activation(out=values[:, rows, :], in_=pre[:], func=func)
+
+        x_reset_t = {}
+        reset_t = {}
+        update = {}
+        cand = {}
+
+        def turn_x_reset(rnd):
+            x_reset_t[rnd] = work.tile([P, COL_TILES, BANK], BF16, name="x_reset_t")
+            for first in range(0, COL_TILES, 2):
+                turned = psum_plain.tile([P, 2, BANK], BF16, tag="plain")
+                for i in range(2):
+                    for j in range(TILES):
+                        nc.tensor.transpose(
+                            turned[:, i, P * j : P * (j + 1)],
+                            x_of(RESET, rnd, j)[:, P * (first + i) : P * (first + i + 1)],
+                            ident_bf16[:],
+                        )
+                nc.scalar.copy(out=x_reset_t[rnd][:, first : first + 2, :], in_=turned[:])
+
+        def reset_gate(rnd):
+            half, col = place(rnd)
+            reset_t[rnd] = work.tile([P, COL_TILES, BANK], F32, name="reset_t")
+            for ct in range(COL_TILES):
+                acc = product_transposed(RESET, half, col + P * ct)
+                nc.vector.tensor_tensor(
+                    out=reset_t[rnd][:, ct, :], in0=acc[:], in1=x_reset_t[rnd][:, ct, :], op=ALU.add
+                )
                 nc.scalar.activation(
-                    out=pre_t[:, ct, :],
-                    in_=acc[:],
-                    func=ACT.Identity,
-                    bias=bias_col[:, tile_of_w : tile_of_w + 1],
+                    out=reset_t[rnd][:, ct, :],
+                    in_=reset_t[rnd][:, ct, :],
+                    func=ACT.Sigmoid,
+                    bias=bias_of(RESET, col + P * ct),
                     scale=1.0,
                 )
-            return pre_t
 
-        def gate_on_nodes(pre_t, gate, half, q):
-            cols = slice(BANK * q, BANK * (q + 1))
-            values = work.tile([P, TILES, BANK], F32, tag="gate_%d" % gate)
-            for j in range(TILES):
-                pre = psum_plain.tile([P, BANK], F32, tag="plain")
-                for ct in range(TILES):
-                    nc.tensor.matmul(
-                        out=pre[:, P * ct : P * (ct + 1)],
-                        lhsT=pre_t[:, ct, P * j : P * (j + 1)],
-                        rhs=ident_f32[:],
-                        is_transpose=True,
-                        start=(ct == 0),
-                        stop=False,
-                    )
-                nc.tensor.matmul(
-                    out=pre[:],
-                    lhsT=ident_bf16[:],
-                    rhs=x_sb[gate, half][:, j, cols],
-                    start=False,
-                    stop=True,
-                )
-                nc.scalar.activation(out=values[:, j, :], in_=pre[:], func=ACT.Sigmoid)
-            return values
-
-        def candidate_recurrent(half, q):
-            col = BANK * q
-            cand = work.tile([P, TILES, BANK], F32, tag="cand")
-            for j in range(TILES):
-                nodes = slice(P * j, P * (j + 1))
-                acc = psum_mx.tile([P, BANK], F32, tag="mx")
-                for g in range(PASSES):
-                    nc.tensor.matmul_mx(
-                        out=acc[:],
-                        lhsT=h_codes[half][:, g, nodes].bitcast(E4M3_X4),
-                        lhsT_scale=h_scales[half][:, g, nodes],
-                        rhs=w_words[CANDIDATE][:, g, 2 * col : 2 * (col + BANK)].bitcast(E2M1_X4),
-                        rhs_scale=w_scales[:, g, HIDDEN * CANDIDATE + col : HIDDEN * CANDIDATE + col + BANK],
-                        start=(g == 0),
-                        stop=(g == PASSES - 1),
-                    )
-                nc.vector.tensor_tensor(
-                    out=cand[:, j, :],
+        def candidate_product(rnd):
+            half, col = place(rnd)
+            for ct in range(COL_TILES):
+                acc = product_transposed(CANDIDATE, half, col + P * ct)
+                nc.vector.scalar_tensor_tensor(
+                    out=reset_t[rnd][:, ct, :],
                     in0=acc[:],
-                    in1=cand_bias[:, BANK * q : BANK * (q + 1)],
-                    op=ALU.add,
+                    scalar=bias_of(CANDIDATE, col + P * ct),
+                    in1=reset_t[rnd][:, ct, :],
+                    op0=ALU.add,
+                    op1=ALU.mult,
                 )
-            return cand
+
+        def candidate_on_nodes(rnd):
+            cand[rnd] = work.tile([P, TILES, ROUND_COLS], F32, name="cand")
+            back_on_nodes(reset_t[rnd], CANDIDATE, rnd, ACT.Tanh, cand[rnd])
+
+        update_t = {}
+
+        def update_product(rnd):
+            half, col = place(rnd)
+            update_t[rnd] = work.tile([P, COL_TILES, BANK], F32, name="update_t")
+            for ct in range(COL_TILES):
+                acc = product_transposed(UPDATE, half, col + P * ct)
+                nc.scalar.activation(
+                    out=update_t[rnd][:, ct, :],
+                    in_=acc[:],
+                    func=ACT.Identity,
+                    bias=bias_of(UPDATE, col + P * ct),
+                    scale=1.0,
+                )
+
+        def update_on_nodes(rnd):
+            update[rnd] = longer.tile([P, TILES, ROUND_COLS], F32, name="update")
+            back_on_nodes(update_t[rnd], UPDATE, rnd, ACT.Sigmoid, update[rnd])
 
         pair_starts = range(0, TILES, 2)
 
-        def candidate_input(cand, reset, half, q):
-            cols = slice(BANK * q, BANK * (q + 1))
-            for first in pair_starts:
-                rows = slice(first, first + 2)
-                nc.vector.tensor_tensor(
-                    out=cand[:, rows, :], in0=cand[:, rows, :], in1=reset[:, rows, :], op=ALU.mult
-                )
-            for first in pair_starts:
-                rows = slice(first, first + 2)
-                nc.vector.tensor_tensor(
-                    out=cand[:, rows, :],
-                    in0=cand[:, rows, :],
-                    in1=x_sb[CANDIDATE, half][:, rows, cols],
-                    op=ALU.add,
-                )
-
-        def squash(cand):
-            for first in pair_starts:
-                rows = slice(first, first + 2)
-                nc.scalar.activation(out=cand[:, rows, :], in_=cand[:, rows, :], func=ACT.Tanh)
-
-        def mix_and_store(cand, update, half, q):
-            cols = slice(BANK * q, BANK * (q + 1))
-            mixed = work.tile([P, TILES, BANK], F32, tag="mixed")
+        def mix_and_store(rnd):
+            half, col = place(rnd)
+            cols = slice(col, col + ROUND_COLS)
+            mixed = longer.tile([P, TILES, ROUND_COLS], F32, name="mixed")
             for first in pair_starts:
                 rows = slice(first, first + 2)
                 tiles = slice(TILES * half + first, TILES * half + first + 2)
                 nc.vector.tensor_tensor(
-                    out=mixed[:, rows, :], in0=h_sb[:, tiles, cols], in1=cand[:, rows, :], op=ALU.subtract
+                    out=mixed[:, rows, :], in0=h_sb[:, tiles, cols], in1=cand[rnd][:, rows, :], op=ALU.subtract
                 )
             for first in pair_starts:
                 rows = slice(first, first + 2)
                 nc.vector.tensor_tensor(
-                    out=mixed[:, rows, :], in0=mixed[:, rows, :], in1=update[:, rows, :], op=ALU.mult
+                    out=mixed[:, rows, :], in0=mixed[:, rows, :], in1=update[rnd][:, rows, :], op=ALU.mult
                 )
             for first in pair_starts:
                 rows = slice(first, first + 2)
                 tiles = slice(TILES * half + first, TILES * half + first + 2)
                 nc.vector.tensor_tensor(
-                    out=mixed[:, rows, :], in0=mixed[:, rows, :], in1=cand[:, rows, :], op=ALU.add
+                    out=mixed[:, rows, :], in0=mixed[:, rows, :], in1=cand[rnd][:, rows, :], op=ALU.add
                 )
                 nc.sync.dma_start(out=out_dram[:, tiles, cols], in_=mixed[:, rows, :])
 
-        for half in range(HALVES):
-            for q in range(COLUMN_HALVES):
-                reset_t = gate_transposed(RESET, half, q)
-                cand = candidate_recurrent(half, q)
-                reset = gate_on_nodes(reset_t, RESET, half, q)
-                update_t = gate_transposed(UPDATE, half, q)
-                candidate_input(cand, reset, half, q)
-                squash(cand)
-                update = gate_on_nodes(update_t, UPDATE, half, q)
-                mix_and_store(cand, update, half, q)
-                if q == 0 and half + 1 < HALVES:
-                    quantise_half(turn_half(half + 1), half + 1)
+        turn_steps = max(1, ROUNDS_PER_HALF - 2)
+        for step in range(-2, ROUNDS + 1):
+            if 0 <= step < ROUNDS:
+                candidate_product(step)
+            if 0 <= step + 1 < ROUNDS:
+                reset_gate(step + 1)
+                update_product(step + 1)
+            if 0 <= step < ROUNDS:
+                candidate_on_nodes(step)
+            if 0 <= step + 2 < ROUNDS:
+                turn_x_reset(step + 2)
+            if 0 <= step + 1 < ROUNDS:
+                update_on_nodes(step + 1)
+            if 0 <= step < turn_steps:
+                for j in range(TILES * step // turn_steps, TILES * (step + 1) // turn_steps):
+                    turn_tile(1, j)
+            if 0 <= step - 1 < ROUNDS:
+                mix_and_store(step - 1)
+            if step == max(turn_steps - 1, ROUNDS_PER_HALF - 3):
+                quantise_half(1)

@@ -51,8 +51,7 @@ def tile_gatedgraphconvolution_pb_kernel(
         stage = stack.enter_context(tc.tile_pool(name="stage", bufs=2))
         work = stack.enter_context(tc.tile_pool(name="work", bufs=2))
         longer = stack.enter_context(tc.tile_pool(name="longer", bufs=3))
-        psum_mx = stack.enter_context(tc.psum_pool(name="psum_mx", bufs=4))
-        psum_plain = stack.enter_context(tc.psum_pool(name="psum_plain", bufs=4))
+        psum = stack.enter_context(tc.psum_pool(name="psum", bufs=8))
 
         h_sb = keep.tile([P, NODE_TILES, HIDDEN], BF16)
         x_sb = {}
@@ -129,7 +128,7 @@ def tile_gatedgraphconvolution_pb_kernel(
             if j == 0:
                 grouped[half] = stage.tile([P, PASSES, BANK, 4], BF16, align_bytes=64, name="grouped")
             grouped_words = grouped[half][:].bitcast(F32)
-            turned = psum_plain.tile([P, PASSES, 2, P], F32, tag="plain")
+            turned = psum.tile([P, PASSES, 2, P], F32, tag="bank")
             for g in range(PASSES):
                 for u in range(2):
                     nc.tensor.transpose(
@@ -153,7 +152,7 @@ def tile_gatedgraphconvolution_pb_kernel(
         for j in range(TILES):
             turn_tile(0, j)
 
-        bias_turned = psum_plain.tile([P, P], BF16, tag="plain")
+        bias_turned = psum.tile([P, P], BF16, tag="bank")
         nc.tensor.transpose(bias_turned[:], bias_rows[:], ident_bf16[:])
         bias_col = keep.tile([P, GATE_COLS // P], F32)
         nc.vector.tensor_copy(out=bias_col[:], in_=bias_turned[:, 0 : GATE_COLS // P])
@@ -172,7 +171,7 @@ def tile_gatedgraphconvolution_pb_kernel(
 
         def product_transposed(gate, half, col):
             in_w = HIDDEN * gate + col
-            acc = psum_mx.tile([P, BANK], F32, tag="mx")
+            acc = psum.tile([P, BANK], F32, tag="bank")
             for g in range(PASSES):
                 nc.tensor.matmul_mx(
                     out=acc[:],
@@ -185,25 +184,41 @@ def tile_gatedgraphconvolution_pb_kernel(
                 )
             return acc
 
-        def back_on_nodes(transposed, gate, rnd, func, values):
+        def open_banks(gate, rnd):
+            half, col = place(rnd)
+            x_block = x_sb[gate, half, col // X_COLS]
+            banks = []
             for bank in range(ROUND_BANKS):
-                pre = psum_plain.tile([P, TILES_PER_BANK, ROUND_COLS], F32, tag="plain")
+                pre = psum.tile([P, TILES_PER_BANK, ROUND_COLS], F32, tag="bank")
+                banks.append(pre)
+                nc.tensor.matmul(
+                    out=pre[:],
+                    lhsT=ident_bf16[:],
+                    rhs=x_block[
+                        :,
+                        TILES_PER_BANK * bank : TILES_PER_BANK * (bank + 1),
+                        col % X_COLS : col % X_COLS + ROUND_COLS,
+                    ],
+                    start=True,
+                    stop=False,
+                )
+            return banks
+
+        def back_on_nodes(transposed, banks, func, values):
+            for bank in range(ROUND_BANKS):
                 for i in range(TILES_PER_BANK):
                     j = TILES_PER_BANK * bank + i
                     for ct in range(COL_TILES):
                         nc.tensor.matmul(
-                            out=pre[:, i, P * ct : P * (ct + 1)],
+                            out=banks[bank][:, i, P * ct : P * (ct + 1)],
                             lhsT=transposed[:, ct, P * j : P * (j + 1)],
                             rhs=ident_f32[:],
                             is_transpose=True,
-                            start=(ct == 0),
-                            stop=False,
+                            start=False,
+                            stop=(i == TILES_PER_BANK - 1 and ct == COL_TILES - 1),
                         )
-                    nc.tensor.matmul(
-                        out=pre[:, i, :], lhsT=ident_bf16[:], rhs=x_of(gate, rnd, j), start=False, stop=True
-                    )
                 rows = slice(TILES_PER_BANK * bank, TILES_PER_BANK * (bank + 1))
-                nc.scalar.activation(out=values[:, rows, :], in_=pre[:], func=func)
+                nc.scalar.activation(out=values[:, rows, :], in_=banks[bank][:], func=func)
 
         x_reset_t = {}
         reset_t = {}
@@ -213,7 +228,7 @@ def tile_gatedgraphconvolution_pb_kernel(
         def turn_x_reset(rnd):
             x_reset_t[rnd] = work.tile([P, COL_TILES, BANK], BF16, name="x_reset_t")
             for first in range(0, COL_TILES, 2):
-                turned = psum_plain.tile([P, 2, BANK], BF16, tag="plain")
+                turned = psum.tile([P, 2, BANK], BF16, tag="bank")
                 for i in range(2):
                     for j in range(TILES):
                         nc.tensor.transpose(
@@ -223,14 +238,18 @@ def tile_gatedgraphconvolution_pb_kernel(
                         )
                 nc.scalar.copy(out=x_reset_t[rnd][:, first : first + 2, :], in_=turned[:])
 
-        def reset_gate(rnd):
+        def reset_gate(rnd, ct):
             half, col = place(rnd)
-            reset_t[rnd] = work.tile([P, COL_TILES, BANK], F32, name="reset_t")
+            if ct == 0:
+                reset_t[rnd] = work.tile([P, COL_TILES, BANK], F32, name="reset_t")
+            acc = product_transposed(RESET, half, col + P * ct)
+            nc.vector.tensor_tensor(
+                out=reset_t[rnd][:, ct, :], in0=acc[:], in1=x_reset_t[rnd][:, ct, :], op=ALU.add
+            )
+
+        def reset_squash(rnd):
+            half, col = place(rnd)
             for ct in range(COL_TILES):
-                acc = product_transposed(RESET, half, col + P * ct)
-                nc.vector.tensor_tensor(
-                    out=reset_t[rnd][:, ct, :], in0=acc[:], in1=x_reset_t[rnd][:, ct, :], op=ALU.add
-                )
                 nc.scalar.activation(
                     out=reset_t[rnd][:, ct, :],
                     in_=reset_t[rnd][:, ct, :],
@@ -239,22 +258,21 @@ def tile_gatedgraphconvolution_pb_kernel(
                     scale=1.0,
                 )
 
-        def candidate_product(rnd):
+        def candidate_product(rnd, ct):
             half, col = place(rnd)
-            for ct in range(COL_TILES):
-                acc = product_transposed(CANDIDATE, half, col + P * ct)
-                nc.vector.scalar_tensor_tensor(
-                    out=reset_t[rnd][:, ct, :],
-                    in0=acc[:],
-                    scalar=bias_of(CANDIDATE, col + P * ct),
-                    in1=reset_t[rnd][:, ct, :],
-                    op0=ALU.add,
-                    op1=ALU.mult,
-                )
+            acc = product_transposed(CANDIDATE, half, col + P * ct)
+            nc.vector.scalar_tensor_tensor(
+                out=reset_t[rnd][:, ct, :],
+                in0=acc[:],
+                scalar=bias_of(CANDIDATE, col + P * ct),
+                in1=reset_t[rnd][:, ct, :],
+                op0=ALU.add,
+                op1=ALU.mult,
+            )
 
-        def candidate_on_nodes(rnd):
+        def candidate_on_nodes(rnd, banks):
             cand[rnd] = work.tile([P, TILES, ROUND_COLS], F32, name="cand")
-            back_on_nodes(reset_t[rnd], CANDIDATE, rnd, ACT.Tanh, cand[rnd])
+            back_on_nodes(reset_t[rnd], banks, ACT.Tanh, cand[rnd])
 
         update_t = {}
 
@@ -271,9 +289,9 @@ def tile_gatedgraphconvolution_pb_kernel(
                     scale=1.0,
                 )
 
-        def update_on_nodes(rnd):
+        def update_on_nodes(rnd, banks):
             update[rnd] = longer.tile([P, TILES, ROUND_COLS], F32, name="update")
-            back_on_nodes(update_t[rnd], UPDATE, rnd, ACT.Sigmoid, update[rnd])
+            back_on_nodes(update_t[rnd], banks, ACT.Sigmoid, update[rnd])
 
         pair_starts = range(0, TILES, 2)
 
@@ -303,16 +321,22 @@ def tile_gatedgraphconvolution_pb_kernel(
         turn_steps = max(1, ROUNDS_PER_HALF - 2)
         for step in range(-2, ROUNDS + 1):
             if 0 <= step < ROUNDS:
-                candidate_product(step)
+                for ct in range(COL_TILES):
+                    candidate_product(step, ct)
             if 0 <= step + 1 < ROUNDS:
-                reset_gate(step + 1)
+                for ct in range(COL_TILES):
+                    reset_gate(step + 1, ct)
                 update_product(step + 1)
+            cand_banks = open_banks(CANDIDATE, step) if 0 <= step < ROUNDS else None
+            update_banks = open_banks(UPDATE, step + 1) if 0 <= step + 1 < ROUNDS else None
             if 0 <= step < ROUNDS:
-                candidate_on_nodes(step)
+                candidate_on_nodes(step, cand_banks)
+            if 0 <= step + 1 < ROUNDS:
+                reset_squash(step + 1)
             if 0 <= step + 2 < ROUNDS:
                 turn_x_reset(step + 2)
             if 0 <= step + 1 < ROUNDS:
-                update_on_nodes(step + 1)
+                update_on_nodes(step + 1, update_banks)
             if 0 <= step < turn_steps:
                 for j in range(TILES * step // turn_steps, TILES * (step + 1) // turn_steps):
                     turn_tile(1, j)

@@ -328,7 +328,6 @@ def tile_gatedgraphconvolution_pb_kernel(
                     reset_gate(step + 1, ct)
                 update_product(step + 1)
             cand_banks = open_banks(CANDIDATE, step) if 0 <= step < ROUNDS else None
-            update_banks = open_banks(UPDATE, step + 1) if 0 <= step + 1 < ROUNDS else None
             if 0 <= step < ROUNDS:
                 candidate_on_nodes(step, cand_banks)
             if 0 <= step + 1 < ROUNDS:
@@ -336,6 +335,7 @@ def tile_gatedgraphconvolution_pb_kernel(
             if 0 <= step + 2 < ROUNDS:
                 turn_x_reset(step + 2)
             if 0 <= step + 1 < ROUNDS:
+                update_banks = open_banks(UPDATE, step + 1)
                 update_on_nodes(step + 1, update_banks)
             if 0 <= step < turn_steps:
                 for j in range(TILES * step // turn_steps, TILES * (step + 1) // turn_steps):

@@ -80,6 +80,15 @@ def tile_gatedgraphconvolution_pb_kernel(
         nc.vector.memset(w_scales[:].bitcast(I32), 0)
         make_identity(nc, ident_f32[:])
         make_identity(nc, ident_bf16[:])
+        zeros = keep.tile([P, BANK], BF16)
+        nc.vector.memset(zeros[:], 0.0)
+        idle_bank = psum.tile([P, BANK], F32, tag="bank")
+
+        def keep_clock_up(moving):
+            for i in range(2):
+                nc.tensor.matmul(out=idle_bank[:], lhsT=ident_bf16[:], rhs=moving, start=True, stop=True)
+
+        keep_clock_up(zeros[:])
 
         def load_w(gate):
             gate_bytes = slice(2 * HIDDEN * gate, 2 * HIDDEN * (gate + 1))
@@ -108,18 +117,18 @@ def tile_gatedgraphconvolution_pb_kernel(
                 )
         load_w(RESET)
         load_x(RESET, 0, 0)
-        load_w(UPDATE)
-        load_x(UPDATE, 0, 0)
         load_w(CANDIDATE)
+        load_w(UPDATE)
         load_x(CANDIDATE, 0, 0)
+        load_x(UPDATE, 0, 0)
         load_x(RESET, 0, 1)
         nc.sync.dma_start(out=h_sb[:, TILES:, :], in_=h_dram[:, TILES:, :])
-        load_x(UPDATE, 0, 1)
         load_x(CANDIDATE, 0, 1)
+        load_x(UPDATE, 0, 1)
         for block in range(HIDDEN // X_COLS):
             load_x(RESET, 1, block)
-            load_x(UPDATE, 1, block)
             load_x(CANDIDATE, 1, block)
+            load_x(UPDATE, 1, block)
 
         h_words = h_sb[:].bitcast(F32)
         grouped = {}
@@ -151,6 +160,8 @@ def tile_gatedgraphconvolution_pb_kernel(
 
         for j in range(TILES):
             turn_tile(0, j)
+        keep_clock_up(zeros[:])
+        keep_clock_up(grouped[0][:, 0, BANK - P :, :].rearrange("p n f -> p (n f)"))
 
         bias_turned = psum.tile([P, P], BF16, tag="bank")
         nc.tensor.transpose(bias_turned[:], bias_rows[:], ident_bf16[:])
@@ -326,7 +337,8 @@ def tile_gatedgraphconvolution_pb_kernel(
             if 0 <= step + 1 < ROUNDS:
                 for ct in range(COL_TILES):
                     reset_gate(step + 1, ct)
-                update_product(step + 1)
+            if 0 <= step < ROUNDS:
+                update_product(step)
             cand_banks = open_banks(CANDIDATE, step) if 0 <= step < ROUNDS else None
             if 0 <= step < ROUNDS:
                 candidate_on_nodes(step, cand_banks)
@@ -334,9 +346,9 @@ def tile_gatedgraphconvolution_pb_kernel(
                 reset_squash(step + 1)
             if 0 <= step + 2 < ROUNDS:
                 turn_x_reset(step + 2)
-            if 0 <= step + 1 < ROUNDS:
-                update_banks = open_banks(UPDATE, step + 1)
-                update_on_nodes(step + 1, update_banks)
+            if 0 <= step < ROUNDS:
+                update_banks = open_banks(UPDATE, step)
+                update_on_nodes(step, update_banks)
             if 0 <= step < turn_steps:
                 for j in range(TILES * step // turn_steps, TILES * (step + 1) // turn_steps):
                     turn_tile(1, j)

@@ -59,9 +59,11 @@ def tile_gatedgraphconvolution_pb_kernel(
         h_codes = {}
         h_scales = {}
         for gate in (UPDATE, RESET, CANDIDATE):
-            w_words[gate] = keep.tile([P, PASSES, 2 * HIDDEN], U8, align_bytes=64, name="w_words_%d" % gate)
-            for half in range(HALVES):
-                for block in range(HIDDEN // X_COLS):
+            for block in range(HIDDEN // X_COLS):
+                w_words[gate, block] = keep.tile(
+                    [P, PASSES, 2 * X_COLS], U8, align_bytes=64, name="w_words_%d_%d" % (gate, block)
+                )
+                for half in range(HALVES):
                     x_sb[gate, half, block] = keep.tile(
                         [P, TILES, X_COLS], BF16, name="x_%d_%d_%d" % (gate, half, block)
                     )
@@ -90,11 +92,13 @@ def tile_gatedgraphconvolution_pb_kernel(
 
         keep_clock_up(zeros[:])
 
-        def load_w(gate):
-            gate_bytes = slice(2 * HIDDEN * gate, 2 * HIDDEN * (gate + 1))
+        def load_w(gate, block):
+            first = 2 * (HIDDEN * gate + X_COLS * block)
             nc.sync.dma_start(
-                out=w_words[gate][:].bitcast(I32),
-                in_=recurrent_kernel_words[:, :, gate_bytes].rearrange("g p b -> p g b").bitcast(I32),
+                out=w_words[gate, block][:].bitcast(I32),
+                in_=recurrent_kernel_words[:, :, first : first + 2 * X_COLS]
+                .rearrange("g p b -> p g b")
+                .bitcast(I32),
             )
 
         def load_x(gate, half, block):
@@ -107,22 +111,23 @@ def tile_gatedgraphconvolution_pb_kernel(
         nc.sync.dma_start(
             out=bias_rows[0 : GATE_COLS // P, :], in_=bias_h.rearrange("(m c) -> m c", c=P)
         )
-        for b in range(2):
-            for r in range(4):
-                nc.sync.dma_start(
-                    out=w_scales[32 * b + r : P : 64, :, :].bitcast(I32),
-                    in_=recurrent_kernel_scales[:, 4 * b + r : 16 : 8, :]
-                    .rearrange("g s n -> s g n")
-                    .bitcast(I32),
-                )
-        load_w(RESET)
+        for r in range(4):
+            nc.sync.dma_start(
+                out=w_scales[r : P : 32, :, :].bitcast(I32),
+                in_=recurrent_kernel_scales[:, r : 16 : 4, :].rearrange("g s n -> s g n").bitcast(I32),
+            )
+        load_w(RESET, 0)
         load_x(RESET, 0, 0)
-        load_w(CANDIDATE)
-        load_w(UPDATE)
+        load_w(CANDIDATE, 0)
+        load_w(UPDATE, 0)
         load_x(CANDIDATE, 0, 0)
         load_x(UPDATE, 0, 0)
         load_x(RESET, 0, 1)
-        nc.sync.dma_start(out=h_sb[:, TILES:, :], in_=h_dram[:, TILES:, :])
+        load_w(RESET, 1)
+        for t in range(TILES, NODE_TILES, 2):
+            nc.sync.dma_start(out=h_sb[:, t : t + 2, :], in_=h_dram[:, t : t + 2, :])
+        load_w(CANDIDATE, 1)
+        load_w(UPDATE, 1)
         load_x(CANDIDATE, 0, 1)
         load_x(UPDATE, 0, 1)
         for block in range(HIDDEN // X_COLS):
@@ -186,7 +191,9 @@ def tile_gatedgraphconvolution_pb_kernel(
             for g in range(PASSES):
                 nc.tensor.matmul_mx(
                     out=acc[:],
-                    lhsT=w_words[gate][:, g, 2 * col : 2 * (col + P)].bitcast(E2M1_X4),
+                    lhsT=w_words[gate, col // X_COLS][
+                        :, g, 2 * (col % X_COLS) : 2 * (col % X_COLS + P)
+                    ].bitcast(E2M1_X4),
                     lhsT_scale=w_scales[:, g, in_w : in_w + P],
                     rhs=h_codes[half][:, g, :].bitcast(E4M3_X4),
                     rhs_scale=h_scales[half][:, g, :],

@@ -139,9 +139,8 @@ def tile_gatedgraphconvolution_pb_kernel(
         grouped = {}
 
         def turn_tile(half, j):
-            if j == 0:
-                grouped[half] = stage.tile([P, PASSES, BANK, 4], BF16, align_bytes=64, name="grouped")
-            grouped_words = grouped[half][:].bitcast(F32)
+            grouped[half, j] = stage.tile([P, PASSES, P, 4], BF16, align_bytes=64, name="grouped_%d" % j)
+            grouped_words = grouped[half, j][:].bitcast(F32)
             turned = psum.tile([P, PASSES, 2, P], F32, tag="bank")
             for g in range(PASSES):
                 for u in range(2):
@@ -150,29 +149,27 @@ def tile_gatedgraphconvolution_pb_kernel(
                         h_words[:, TILES * half + j, WORDS * g + u : WORDS * (g + 1) : 2],
                         ident_f32[:],
                     )
-            nc.scalar.copy(
-                out=grouped_words[:, :, P * j : P * (j + 1), :],
-                in_=turned[:].rearrange("p g u m -> p g m u"),
-            )
+            nc.scalar.copy(out=grouped_words, in_=turned[:].rearrange("p g u m -> p g m u"))
 
-        def quantise_half(half):
+        def quantise(half, j):
+            nodes = slice(P * j, P * (j + 1))
             for g in range(PASSES):
                 nc.vector.quantize_mx(
-                    out=h_codes[half][:, g, :].bitcast(E4M3_X4),
-                    scales=h_scales[half][:, g, :],
-                    in_=grouped[half][:, g, :, :].rearrange("p n f -> p (n f)"),
+                    out=h_codes[half][:, g, nodes].bitcast(E4M3_X4),
+                    scales=h_scales[half][:, g, nodes],
+                    in_=grouped[half, j][:, g, :, :].rearrange("p n f -> p (n f)"),
                 )
 
         for j in range(TILES):
             turn_tile(0, j)
+            quantise(0, j)
         keep_clock_up(zeros[:])
-        keep_clock_up(grouped[0][:, 0, BANK - P :, :].rearrange("p n f -> p (n f)"))
+        keep_clock_up(grouped[0, TILES - 1][:, 0, :, :].rearrange("p n f -> p (n f)"))
 
         bias_turned = psum.tile([P, P], BF16, tag="bank")
         nc.tensor.transpose(bias_turned[:], bias_rows[:], ident_bf16[:])
         bias_col = keep.tile([P, GATE_COLS // P], F32)
         nc.vector.tensor_copy(out=bias_col[:], in_=bias_turned[:, 0 : GATE_COLS // P])
-        quantise_half(0)
 
         def place(rnd):
             return rnd // ROUNDS_PER_HALF, ROUND_COLS * (rnd % ROUNDS_PER_HALF)
@@ -362,4 +359,5 @@ def tile_gatedgraphconvolution_pb_kernel(
             if 0 <= step - 1 < ROUNDS:
                 mix_and_store(step - 1)
             if step == max(turn_steps - 1, ROUNDS_PER_HALF - 3):
-                quantise_half(1)
+                for j in range(TILES):
+                    quantise(1, j)

@@ -341,6 +341,9 @@ def tile_gatedgraphconvolution_pb_kernel(
             if 0 <= step + 1 < ROUNDS:
                 for ct in range(COL_TILES):
                     reset_gate(step + 1, ct)
+            if step == turn_steps:
+                for j in range(TILES // 2, TILES):
+                    quantise(1, j)
             if 0 <= step < ROUNDS:
                 update_product(step)
             cand_banks = open_banks(CANDIDATE, step) if 0 <= step < ROUNDS else None
@@ -358,6 +361,6 @@ def tile_gatedgraphconvolution_pb_kernel(
                     turn_tile(1, j)
             if 0 <= step - 1 < ROUNDS:
                 mix_and_store(step - 1)
-            if step == max(turn_steps - 1, ROUNDS_PER_HALF - 3):
-                for j in range(TILES):
+            if step == turn_steps - 1:
+                for j in range(TILES // 2):
                     quantise(1, j)

@@ -310,28 +310,34 @@ def tile_gatedgraphconvolution_pb_kernel(
 
         pair_starts = range(0, TILES, 2)
 
-        def mix_and_store(rnd):
+        mixed = {}
+
+        def mix_start(rnd):
             half, col = place(rnd)
             cols = slice(col, col + ROUND_COLS)
-            mixed = longer.tile([P, TILES, ROUND_COLS], F32, name="mixed")
+            mixed[rnd] = longer.tile([P, TILES, ROUND_COLS], F32, name="mixed")
             for first in pair_starts:
                 rows = slice(first, first + 2)
                 tiles = slice(TILES * half + first, TILES * half + first + 2)
                 nc.vector.tensor_tensor(
-                    out=mixed[:, rows, :], in0=h_sb[:, tiles, cols], in1=cand[rnd][:, rows, :], op=ALU.subtract
+                    out=mixed[rnd][:, rows, :], in0=h_sb[:, tiles, cols], in1=cand[rnd][:, rows, :], op=ALU.subtract
                 )
+
+        def mix_end_and_store(rnd):
+            half, col = place(rnd)
+            cols = slice(col, col + ROUND_COLS)
             for first in pair_starts:
                 rows = slice(first, first + 2)
                 nc.vector.tensor_tensor(
-                    out=mixed[:, rows, :], in0=mixed[:, rows, :], in1=update[rnd][:, rows, :], op=ALU.mult
+                    out=mixed[rnd][:, rows, :], in0=mixed[rnd][:, rows, :], in1=update[rnd][:, rows, :], op=ALU.mult
                 )
             for first in pair_starts:
                 rows = slice(first, first + 2)
                 tiles = slice(TILES * half + first, TILES * half + first + 2)
                 nc.vector.tensor_tensor(
-                    out=mixed[:, rows, :], in0=mixed[:, rows, :], in1=cand[rnd][:, rows, :], op=ALU.add
+                    out=mixed[rnd][:, rows, :], in0=mixed[rnd][:, rows, :], in1=cand[rnd][:, rows, :], op=ALU.add
                 )
-                nc.sync.dma_start(out=out_dram[:, tiles, cols], in_=mixed[:, rows, :])
+                nc.sync.dma_start(out=out_dram[:, tiles, cols], in_=mixed[rnd][:, rows, :])
 
         turn_steps = max(1, ROUNDS_PER_HALF - 2)
         for step in range(-2, ROUNDS + 1):
@@ -360,7 +366,9 @@ def tile_gatedgraphconvolution_pb_kernel(
                 for j in range(TILES * step // turn_steps, TILES * (step + 1) // turn_steps):
                     turn_tile(1, j)
             if 0 <= step - 1 < ROUNDS:
-                mix_and_store(step - 1)
+                mix_end_and_store(step - 1)
+            if 0 <= step < ROUNDS:
+                mix_start(step)
             if step == turn_steps - 1:
                 for j in range(TILES // 2):
                     quantise(1, j)

@@ -70,7 +70,12 @@ def tile_gatedgraphconvolution_pb_kernel(
         for half in range(HALVES):
             h_codes[half] = keep.tile([P, PASSES, BANK], U32, align_bytes=64, name="h_codes_%d" % half)
             h_scales[half] = keep.tile([P, PASSES, BANK], U8, align_bytes=64, name="h_scales_%d" % half)
-        w_scales = keep.tile([P, PASSES, GATE_COLS], U8, align_bytes=64)
+        w_scales = {}
+        for gate in (RESET, CANDIDATE, UPDATE):
+            for block in range(HIDDEN // X_COLS):
+                w_scales[gate, block] = keep.tile(
+                    [P, PASSES, X_COLS], U8, align_bytes=64, name="w_scales_%d_%d" % (gate, block)
+                )
         bias_rows = keep.tile([P, P], BF16)
         ident_f32 = keep.tile([P, P], F32)
         ident_bf16 = keep.tile([P, P], BF16)
@@ -79,7 +84,9 @@ def tile_gatedgraphconvolution_pb_kernel(
         nc.vector.memset(table_warmer[:], 0.0)
         nc.scalar.activation(out=table_warmer[:], in_=table_warmer[:], func=ACT.Sigmoid)
         nc.vector.memset(bias_rows[:], 0.0)
-        nc.vector.memset(w_scales[:].bitcast(I32), 0)
+        for block in range(HIDDEN // X_COLS):
+            for gate in (RESET, CANDIDATE, UPDATE):
+                nc.vector.memset(w_scales[gate, block][:].bitcast(I32), 0)
         make_identity(nc, ident_f32[:])
         make_identity(nc, ident_bf16[:])
         zeros = keep.tile([P, BANK], BF16)
@@ -93,6 +100,14 @@ def tile_gatedgraphconvolution_pb_kernel(
         keep_clock_up(zeros[:])
 
         def load_w(gate, block):
+            first = HIDDEN * gate + X_COLS * block
+            for r in range(4):
+                nc.sync.dma_start(
+                    out=w_scales[gate, block][r : P : 32, :, :].bitcast(I32),
+                    in_=recurrent_kernel_scales[:, r : 16 : 4, first : first + X_COLS]
+                    .rearrange("g s n -> s g n")
+                    .bitcast(I32),
+                )
             first = 2 * (HIDDEN * gate + X_COLS * block)
             nc.sync.dma_start(
                 out=w_words[gate, block][:].bitcast(I32),
@@ -111,11 +126,6 @@ def tile_gatedgraphconvolution_pb_kernel(
         nc.sync.dma_start(
             out=bias_rows[0 : GATE_COLS // P, :], in_=bias_h.rearrange("(m c) -> m c", c=P)
         )
-        for r in range(4):
-            nc.sync.dma_start(
-                out=w_scales[r : P : 32, :, :].bitcast(I32),
-                in_=recurrent_kernel_scales[:, r : 16 : 4, :].rearrange("g s n -> s g n").bitcast(I32),
-            )
         load_w(RESET, 0)
         load_x(RESET, 0, 0)
         load_w(CANDIDATE, 0)
@@ -183,7 +193,6 @@ def tile_gatedgraphconvolution_pb_kernel(
             return bias_col[:, tile_of_w : tile_of_w + 1]
 
         def product_transposed(gate, half, col):
-            in_w = HIDDEN * gate + col
             acc = psum.tile([P, BANK], F32, tag="bank")
             for g in range(PASSES):
                 nc.tensor.matmul_mx(
@@ -191,7 +200,7 @@ def tile_gatedgraphconvolution_pb_kernel(
                     lhsT=w_words[gate, col // X_COLS][
                         :, g, 2 * (col % X_COLS) : 2 * (col % X_COLS + P)
                     ].bitcast(E2M1_X4),
-                    lhsT_scale=w_scales[:, g, in_w : in_w + P],
+                    lhsT_scale=w_scales[gate, col // X_COLS][:, g, col % X_COLS : col % X_COLS + P],
                     rhs=h_codes[half][:, g, :].bitcast(E4M3_X4),
                     rhs_scale=h_scales[half][:, g, :],
                     start=(g == 0),

@@ -97,8 +97,6 @@ def tile_gatedgraphconvolution_pb_kernel(
             for i in range(2):
                 nc.tensor.matmul(out=idle_bank[:], lhsT=ident_bf16[:], rhs=moving, start=True, stop=True)
 
-        keep_clock_up(zeros[:])
-
         def load_w(gate, block):
             first = HIDDEN * gate + X_COLS * block
             for r in range(4):
@@ -173,6 +171,7 @@ def tile_gatedgraphconvolution_pb_kernel(
         for j in range(TILES):
             turn_tile(0, j)
             quantise(0, j)
+        keep_clock_up(zeros[:])
         keep_clock_up(zeros[:])
         keep_clock_up(grouped[0, TILES - 1][:, 0, :, :].rearrange("p n f -> p (n f)"))
 

from contextlib import ExitStack

import concourse.mybir as mybir
from concourse.masks import make_identity

F32 = mybir.dt.float32
BF16 = mybir.dt.bfloat16
I32 = mybir.dt.int32
U8 = mybir.dt.uint8
U32 = mybir.dt.uint32
E4M3_X4 = mybir.dt.float8_e4m3fn_x4
E2M1_X4 = mybir.dt.float4_e2m1fn_x4
ACT = mybir.ActivationFunctionType
ALU = mybir.AluOpType

P = 128
NODES = 1024
HIDDEN = 1024
GATE_COLS = 3 * HIDDEN
UPDATE, RESET, CANDIDATE = 0, 1, 2
K_PASS = 4 * P
PASSES = HIDDEN // K_PASS
NODE_TILES = NODES // P
BANK = 512
TILES = BANK // P
HALVES = NODES // BANK
WORDS = K_PASS // 2
X_COLS = 512

COL_TILES = 2
ROUND_COLS = P * COL_TILES
ROUNDS_PER_HALF = HIDDEN // ROUND_COLS
ROUNDS = HALVES * ROUNDS_PER_HALF
TILES_PER_BANK = BANK // ROUND_COLS
ROUND_BANKS = TILES // TILES_PER_BANK

FLOPS = 2 * NODES * HIDDEN * GATE_COLS


def tile_gatedgraphconvolution_pb_kernel(
    tc, x_proj, annotations, recurrent_kernel_words, recurrent_kernel_scales, bias_h, out
):
    nc = tc.nc
    x_dram = x_proj.rearrange("(p t) c -> p t c", t=NODE_TILES)
    h_dram = annotations.flatten_outer_dims().rearrange("(p t) k -> p t k", t=NODE_TILES)
    out_dram = out.flatten_outer_dims().rearrange("(p t) c -> p t c", t=NODE_TILES)

    with ExitStack() as stack:
        stack.enter_context(tc.manual_schedule())
        keep = stack.enter_context(tc.tile_pool(name="keep", bufs=1))
        stage = stack.enter_context(tc.tile_pool(name="stage", bufs=2))
        work = stack.enter_context(tc.tile_pool(name="work", bufs=2))
        longer = stack.enter_context(tc.tile_pool(name="longer", bufs=3))
        psum = stack.enter_context(tc.psum_pool(name="psum", bufs=8))

        h_sb = keep.tile([P, NODE_TILES, HIDDEN], BF16)
        x_sb = {}
        w_words = {}
        h_codes = {}
        h_scales = {}
        for gate in (UPDATE, RESET, CANDIDATE):
            for block in range(HIDDEN // X_COLS):
                w_words[gate, block] = keep.tile(
                    [P, PASSES, 2 * X_COLS], U8, align_bytes=64, name="w_words_%d_%d" % (gate, block)
                )
                for half in range(HALVES):
                    x_sb[gate, half, block] = keep.tile(
                        [P, TILES, X_COLS], BF16, name="x_%d_%d_%d" % (gate, half, block)
                    )
        for half in range(HALVES):
            h_codes[half] = keep.tile([P, PASSES, BANK], U32, align_bytes=64, name="h_codes_%d" % half)
            h_scales[half] = keep.tile([P, PASSES, BANK], U8, align_bytes=64, name="h_scales_%d" % half)
        w_scales = {}
        for gate in (RESET, CANDIDATE, UPDATE):
            for block in range(HIDDEN // X_COLS):
                w_scales[gate, block] = keep.tile(
                    [P, PASSES, X_COLS], U8, align_bytes=64, name="w_scales_%d_%d" % (gate, block)
                )
        bias_rows = keep.tile([P, P], BF16)
        ident_f32 = keep.tile([P, P], F32)
        ident_bf16 = keep.tile([P, P], BF16)

        table_warmer = keep.tile([P, 1], F32)
        nc.vector.memset(table_warmer[:], 0.0)
        nc.scalar.activation(out=table_warmer[:], in_=table_warmer[:], func=ACT.Sigmoid)
        nc.vector.memset(bias_rows[:], 0.0)
        for block in range(HIDDEN // X_COLS):
            for gate in (RESET, CANDIDATE, UPDATE):
                nc.vector.memset(w_scales[gate, block][:].bitcast(I32), 0)
        make_identity(nc, ident_f32[:])
        make_identity(nc, ident_bf16[:])
        zeros = keep.tile([P, BANK], BF16)
        nc.vector.memset(zeros[:], 0.0)
        idle_bank = psum.tile([P, BANK], F32, tag="bank")

        def keep_clock_up(moving):
            for i in range(2):
                nc.tensor.matmul(out=idle_bank[:], lhsT=ident_bf16[:], rhs=moving, start=True, stop=True)

        def load_w(gate, block):
            first = HIDDEN * gate + X_COLS * block
            for r in range(4):
                nc.sync.dma_start(
                    out=w_scales[gate, block][r : P : 32, :, :].bitcast(I32),
                    in_=recurrent_kernel_scales[:, r : 16 : 4, first : first + X_COLS]
                    .rearrange("g s n -> s g n")
                    .bitcast(I32),
                )
            first = 2 * (HIDDEN * gate + X_COLS * block)
            nc.sync.dma_start(
                out=w_words[gate, block][:].bitcast(I32),
                in_=recurrent_kernel_words[:, :, first : first + 2 * X_COLS]
                .rearrange("g p b -> p g b")
                .bitcast(I32),
            )

        def load_x(gate, half, block):
            tiles = slice(TILES * half, TILES * (half + 1))
            first = HIDDEN * gate + X_COLS * block
            nc.sync.dma_start(out=x_sb[gate, half, block][:], in_=x_dram[:, tiles, first : first + X_COLS])

        for t in range(TILES):
            nc.sync.dma_start(out=h_sb[:, t, :], in_=h_dram[:, t, :])
        nc.sync.dma_start(
            out=bias_rows[0 : GATE_COLS // P, :], in_=bias_h.rearrange("(m c) -> m c", c=P)
        )
        load_w(RESET, 0)
        load_x(RESET, 0, 0)
        load_w(CANDIDATE, 0)
        load_w(UPDATE, 0)
        load_x(CANDIDATE, 0, 0)
        load_x(UPDATE, 0, 0)
        load_x(RESET, 0, 1)
        load_w(RESET, 1)
        for t in range(TILES, NODE_TILES, 2):
            nc.sync.dma_start(out=h_sb[:, t : t + 2, :], in_=h_dram[:, t : t + 2, :])
        load_w(CANDIDATE, 1)
        load_w(UPDATE, 1)
        load_x(CANDIDATE, 0, 1)
        load_x(UPDATE, 0, 1)
        for block in range(HIDDEN // X_COLS):
            load_x(RESET, 1, block)
            load_x(CANDIDATE, 1, block)
            load_x(UPDATE, 1, block)

        h_words = h_sb[:].bitcast(F32)
        grouped = {}

        def turn_tile(half, j):
            grouped[half, j] = stage.tile([P, PASSES, P, 4], BF16, align_bytes=64, name="grouped_%d" % j)
            grouped_words = grouped[half, j][:].bitcast(F32)
            turned = psum.tile([P, PASSES, 2, P], F32, tag="bank")
            for g in range(PASSES):
                for u in range(2):
                    nc.tensor.transpose(
                        turned[:, g, u, :],
                        h_words[:, TILES * half + j, WORDS * g + u : WORDS * (g + 1) : 2],
                        ident_f32[:],
                    )
            nc.scalar.copy(out=grouped_words, in_=turned[:].rearrange("p g u m -> p g m u"))

        def quantise(half, j):
            nodes = slice(P * j, P * (j + 1))
            for g in range(PASSES):
                nc.vector.quantize_mx(
                    out=h_codes[half][:, g, nodes].bitcast(E4M3_X4),
                    scales=h_scales[half][:, g, nodes],
                    in_=grouped[half, j][:, g, :, :].rearrange("p n f -> p (n f)"),
                )

        for j in range(TILES):
            turn_tile(0, j)
            quantise(0, j)
        keep_clock_up(zeros[:])
        keep_clock_up(zeros[:])
        keep_clock_up(grouped[0, TILES - 1][:, 0, :, :].rearrange("p n f -> p (n f)"))

        bias_turned = psum.tile([P, P], BF16, tag="bank")
        nc.tensor.transpose(bias_turned[:], bias_rows[:], ident_bf16[:])
        bias_col = keep.tile([P, GATE_COLS // P], F32)
        nc.vector.tensor_copy(out=bias_col[:], in_=bias_turned[:, 0 : GATE_COLS // P])

        def place(rnd):
            return rnd // ROUNDS_PER_HALF, ROUND_COLS * (rnd % ROUNDS_PER_HALF)

        def x_of(gate, rnd, j):
            half, col = place(rnd)
            return x_sb[gate, half, col // X_COLS][:, j, col % X_COLS : col % X_COLS + ROUND_COLS]

        def bias_of(gate, col):
            tile_of_w = (HIDDEN * gate + col) // P
            return bias_col[:, tile_of_w : tile_of_w + 1]

        def product_transposed(gate, half, col):
            acc = psum.tile([P, BANK], F32, tag="bank")
            for g in range(PASSES):
                nc.tensor.matmul_mx(
                    out=acc[:],
                    lhsT=w_words[gate, col // X_COLS][
                        :, g, 2 * (col % X_COLS) : 2 * (col % X_COLS + P)
                    ].bitcast(E2M1_X4),
                    lhsT_scale=w_scales[gate, col // X_COLS][:, g, col % X_COLS : col % X_COLS + P],
                    rhs=h_codes[half][:, g, :].bitcast(E4M3_X4),
                    rhs_scale=h_scales[half][:, g, :],
                    start=(g == 0),
                    stop=(g == PASSES - 1),
                )
            return acc

        def open_banks(gate, rnd):
            half, col = place(rnd)
            x_block = x_sb[gate, half, col // X_COLS]
            banks = []
            for bank in range(ROUND_BANKS):
                pre = psum.tile([P, TILES_PER_BANK, ROUND_COLS], F32, tag="bank")
                banks.append(pre)
                nc.tensor.matmul(
                    out=pre[:],
                    lhsT=ident_bf16[:],
                    rhs=x_block[
                        :,
                        TILES_PER_BANK * bank : TILES_PER_BANK * (bank + 1),
                        col % X_COLS : col % X_COLS + ROUND_COLS,
                    ],
                    start=True,
                    stop=False,
                )
            return banks

        def back_on_nodes(transposed, banks, func, values):
            for bank in range(ROUND_BANKS):
                for i in range(TILES_PER_BANK):
                    j = TILES_PER_BANK * bank + i
                    for ct in range(COL_TILES):
                        nc.tensor.matmul(
                            out=banks[bank][:, i, P * ct : P * (ct + 1)],
                            lhsT=transposed[:, ct, P * j : P * (j + 1)],
                            rhs=ident_f32[:],
                            is_transpose=True,
                            start=False,
                            stop=(i == TILES_PER_BANK - 1 and ct == COL_TILES - 1),
                        )
                rows = slice(TILES_PER_BANK * bank, TILES_PER_BANK * (bank + 1))
                nc.scalar.activation(out=values[:, rows, :], in_=banks[bank][:], func=func)

        x_reset_t = {}
        reset_t = {}
        update = {}
        cand = {}

        def turn_x_reset(rnd):
            x_reset_t[rnd] = work.tile([P, COL_TILES, BANK], BF16, name="x_reset_t")
            for first in range(0, COL_TILES, 2):
                turned = psum.tile([P, 2, BANK], BF16, tag="bank")
                for i in range(2):
                    for j in range(TILES):
                        nc.tensor.transpose(
                            turned[:, i, P * j : P * (j + 1)],
                            x_of(RESET, rnd, j)[:, P * (first + i) : P * (first + i + 1)],
                            ident_bf16[:],
                        )
                nc.scalar.copy(out=x_reset_t[rnd][:, first : first + 2, :], in_=turned[:])

        def reset_gate(rnd, ct):
            half, col = place(rnd)
            if ct == 0:
                reset_t[rnd] = work.tile([P, COL_TILES, BANK], F32, name="reset_t")
            acc = product_transposed(RESET, half, col + P * ct)
            nc.vector.tensor_tensor(
                out=reset_t[rnd][:, ct, :], in0=acc[:], in1=x_reset_t[rnd][:, ct, :], op=ALU.add
            )

        def reset_squash(rnd):
            half, col = place(rnd)
            for ct in range(COL_TILES):
                nc.scalar.activation(
                    out=reset_t[rnd][:, ct, :],
                    in_=reset_t[rnd][:, ct, :],
                    func=ACT.Sigmoid,
                    bias=bias_of(RESET, col + P * ct),
                    scale=1.0,
                )

        def candidate_product(rnd, ct):
            half, col = place(rnd)
            acc = product_transposed(CANDIDATE, half, col + P * ct)
            nc.vector.scalar_tensor_tensor(
                out=reset_t[rnd][:, ct, :],
                in0=acc[:],
                scalar=bias_of(CANDIDATE, col + P * ct),
                in1=reset_t[rnd][:, ct, :],
                op0=ALU.add,
                op1=ALU.mult,
            )

        def candidate_on_nodes(rnd, banks):
            cand[rnd] = work.tile([P, TILES, ROUND_COLS], F32, name="cand")
            back_on_nodes(reset_t[rnd], banks, ACT.Tanh, cand[rnd])

        update_t = {}

        def update_product(rnd):
            half, col = place(rnd)
            update_t[rnd] = work.tile([P, COL_TILES, BANK], F32, name="update_t")
            for ct in range(COL_TILES):
                acc = product_transposed(UPDATE, half, col + P * ct)
                nc.scalar.activation(
                    out=update_t[rnd][:, ct, :],
                    in_=acc[:],
                    func=ACT.Identity,
                    bias=bias_of(UPDATE, col + P * ct),
                    scale=1.0,
                )

        def update_on_nodes(rnd, banks):
            update[rnd] = longer.tile([P, TILES, ROUND_COLS], F32, name="update")
            back_on_nodes(update_t[rnd], banks, ACT.Sigmoid, update[rnd])

        pair_starts = range(0, TILES, 2)

        mixed = {}

        def mix_start(rnd):
            half, col = place(rnd)
            cols = slice(col, col + ROUND_COLS)
            mixed[rnd] = longer.tile([P, TILES, ROUND_COLS], F32, name="mixed")
            for first in pair_starts:
                rows = slice(first, first + 2)
                tiles = slice(TILES * half + first, TILES * half + first + 2)
                nc.vector.tensor_tensor(
                    out=mixed[rnd][:, rows, :], in0=h_sb[:, tiles, cols], in1=cand[rnd][:, rows, :], op=ALU.subtract
                )

        def mix_end_and_store(rnd):
            half, col = place(rnd)
            cols = slice(col, col + ROUND_COLS)
            for first in pair_starts:
                rows = slice(first, first + 2)
                nc.vector.tensor_tensor(
                    out=mixed[rnd][:, rows, :], in0=mixed[rnd][:, rows, :], in1=update[rnd][:, rows, :], op=ALU.mult
                )
            for first in pair_starts:
                rows = slice(first, first + 2)
                tiles = slice(TILES * half + first, TILES * half + first + 2)
                nc.vector.tensor_tensor(
                    out=mixed[rnd][:, rows, :], in0=mixed[rnd][:, rows, :], in1=cand[rnd][:, rows, :], op=ALU.add
                )
                nc.sync.dma_start(out=out_dram[:, tiles, cols], in_=mixed[rnd][:, rows, :])

        turn_steps = max(1, ROUNDS_PER_HALF - 2)
        for step in range(-2, ROUNDS + 1):
            if 0 <= step < ROUNDS:
                for ct in range(COL_TILES):
                    candidate_product(step, ct)
            if 0 <= step + 1 < ROUNDS:
                for ct in range(COL_TILES):
                    reset_gate(step + 1, ct)
            if step == turn_steps:
                for j in range(TILES // 2, TILES):
                    quantise(1, j)
            if 0 <= step < ROUNDS:
                update_product(step)
            cand_banks = open_banks(CANDIDATE, step) if 0 <= step < ROUNDS else None
            if 0 <= step < ROUNDS:
                candidate_on_nodes(step, cand_banks)
            if 0 <= step + 1 < ROUNDS:
                reset_squash(step + 1)
            if 0 <= step + 2 < ROUNDS:
                turn_x_reset(step + 2)
            if 0 <= step < ROUNDS:
                update_banks = open_banks(UPDATE, step)
                update_on_nodes(step, update_banks)
            if 0 <= step < turn_steps:
                for j in range(TILES * step // turn_steps, TILES * (step + 1) // turn_steps):
                    turn_tile(1, j)
            if 0 <= step - 1 < ROUNDS:
                mix_end_and_store(step - 1)
            if 0 <= step < ROUNDS:
                mix_start(step)
            if step == turn_steps - 1:
                for j in range(TILES // 2):
                    quantise(1, j)
